import numpy as np
import ml_dtypes


BF16 = ml_dtypes.bfloat16


def bf(x):
    return np.asarray(x, np.float32).astype(BF16)


def f64(x):
    return np.asarray(x).astype(np.float64)


E2M1 = np.array([0.0, 0.5, 1.0, 1.5, 2.0, 3.0, 4.0, 6.0, -0.0, -0.5, -1.0, -1.5, -2.0, -3.0, -4.0, -6.0])


def pack_weight(w, fmt):
    k, n = w.shape
    w = f64(bf(w)).reshape(k // 32, 32, n)
    amax = np.abs(w).max(1)
    if fmt == "e4m3":
        byte = np.frexp(amax)[1] - 1 + 127 - 7
    else:
        mant, ex = np.frexp(amax / 6.0)
        byte = np.where(mant > 0.5, ex, ex - 1) + 127
    byte = np.clip(np.where(amax > 0, byte, 1), 1, 254)
    scaled = (w * np.exp2(127.0 - byte)[:, None, :]).reshape(k, n).astype(np.float32)
    by_word = np.ascontiguousarray(scaled.reshape(k // 512, 128, 4, n).transpose(0, 1, 3, 2))
    if fmt == "e4m3":
        words = by_word.astype(ml_dtypes.float8_e4m3fn).view(np.uint8)
    else:
        c = by_word.astype(ml_dtypes.float4_e2m1fn).view(np.uint8) & 0xF
        words = c[..., 0::2] | (c[..., 1::2] << 4)
    return np.ascontiguousarray(words), np.ascontiguousarray(byte.astype(np.uint8).reshape(k // 512, 16, n))


def unpack_weight(words, scales, fmt):
    g, p, n, _ = words.shape
    if fmt == "e4m3":
        vals = np.ascontiguousarray(words).view(ml_dtypes.float8_e4m3fn).astype(np.float64)
    else:
        nib = np.empty((g, p, n, 4), np.uint8)
        nib[..., 0::2] = words & 0xF
        nib[..., 1::2] = words >> 4
        vals = E2M1[nib]
    vals = vals * np.repeat(np.exp2(scales.astype(np.float64) - 127.0), 8, axis=1)[..., None]
    return vals.transpose(0, 1, 3, 2).reshape(g * 512, n)

def pack4(w):
    words, scales = pack_weight(w, "e2m1")
    return words.reshape(words.shape[0], 128, -1), scales


def unpack4(words, scales):
    return unpack_weight(words.reshape(words.shape[0], 128, -1, 2), scales, "e2m1")


def kspread(k):
    return np.exp2(np.repeat(np.random.randint(-6, 7, k // 32), 32).astype(np.float64))


B, D_IN, D_H = 512, 4096, 4096


def sigmoid(v):
    return 1.0 / (1.0 + np.exp(-v))


def setup_inputs():
    s, t = kspread(D_IN), kspread(D_H)
    fg = np.exp(0.75 * np.random.standard_normal((B, D_H)))
    ig = np.exp(0.75 * np.random.standard_normal((B, D_H)))
    c = fg * np.random.standard_normal((B, D_H)) + ig * np.tanh(0.75 * np.random.standard_normal((B, D_H)))
    n = fg * np.random.uniform(size=(B, D_H)) + ig
    x_words, x_scales = pack4((np.random.standard_normal((B, D_IN)) * s).T)
    h_prev_words, h_prev_scales = pack4((np.random.standard_normal((B, D_H)) * t).T)
    W_o_words, W_o_scales = pack4(np.random.standard_normal((D_IN, D_H)) * 0.5 / np.sqrt(D_IN) / s[:, None])
    b_o = bf(np.random.standard_normal(D_H) * 0.3)
    U_o_words, U_o_scales = pack4(np.random.standard_normal((D_H, D_H)) * 0.5 / np.sqrt(D_H) / t[:, None])
    return {"x_words": x_words,
            "x_scales": x_scales,
            "h_prev_words": h_prev_words,
            "h_prev_scales": h_prev_scales,
            "c": bf(c),
            "n": bf(n),
            "W_o_words": W_o_words,
            "W_o_scales": W_o_scales,
            "b_o": b_o,
            "U_o_words": U_o_words,
            "U_o_scales": U_o_scales}


def reference(x_words, x_scales, h_prev_words, h_prev_scales, c, n, W_o_words, W_o_scales, b_o, U_o_words, U_o_scales):
    o = sigmoid((unpack4(x_words, x_scales).T @ unpack4(W_o_words, W_o_scales)) + f64(b_o) + (unpack4(h_prev_words, h_prev_scales).T @ unpack4(U_o_words, U_o_scales)))
    return o * (f64(c) / (f64(n) + 1e-6))

@@ -1,0 +1,219 @@
+from contextlib import ExitStack
+
+import concourse.mybir as mybir
+
+F32 = mybir.dt.float32
+BF16 = mybir.dt.bfloat16
+U8 = mybir.dt.uint8
+I32 = mybir.dt.int32
+FP4X4 = mybir.dt.float4_e2m1fn_x4
+ADD = mybir.AluOpType.add
+MULT = mybir.AluOpType.mult
+ACT = mybir.ActivationFunctionType
+
+P = 128
+TOKENS = 512
+D = 4096
+G = 8
+T_TILES = TOKENS // P
+BANK = 512
+SUPER = 1024
+HALVES = SUPER // BANK
+N_SUPER = D // SUPER
+EPS = 1e-6
+WARM_UP = 9
+FLOPS = 2 * TOKENS * D * (2 * D)
+
+
+def tile_slstmcell_pb_kernel(tc, x_words, x_scales, h_words, h_scales, c, n, w_words, w_scales, b_o, u_words, u_scales, out):
+    nc = tc.nc
+    with ExitStack() as ctx:
+        keep = ctx.enter_context(tc.tile_pool(name="keep", bufs=1))
+        cn_pool = ctx.enter_context(tc.tile_pool(name="cn", bufs=2))
+        y_pool = ctx.enter_context(tc.tile_pool(name="y", bufs=4))
+        ratio_pool = ctx.enter_context(tc.tile_pool(name="ratio", bufs=8))
+        v_pool = ctx.enter_context(tc.tile_pool(name="v", bufs=4))
+        psum = ctx.enter_context(tc.psum_pool(name="psum", bufs=8))
+
+        act_words = (x_words, h_words)
+        act_scales = (x_scales, h_scales)
+        wt_words = (w_words, u_words)
+        wt_scales = (w_scales, u_scales)
+        act_codes, act_planes, wt_codes, wt_planes = [], [], [], []
+        for m in range(2):
+            act_codes.append(keep.tile([P, G, 2 * TOKENS], U8, name="act_codes%d" % m, align_bytes=64))
+            act_planes.append(keep.tile([P, G, TOKENS], U8, name="act_planes%d" % m, align_bytes=64))
+        for b in range(2):
+            codes_b, planes_b = [], []
+            for m in range(2):
+                codes_b.append(keep.tile([P, G, 2 * SUPER], U8, name="wt_codes%d_%d" % (b, m), align_bytes=64))
+                planes_b.append(keep.tile([P, G, SUPER], U8, name="wt_planes%d_%d" % (b, m), align_bytes=64))
+            wt_codes.append(codes_b)
+            wt_planes.append(planes_b)
+        bias_all = keep.tile([P, D], BF16, name="bias_all", align_bytes=64)
+        zeros = keep.tile([P, BANK], BF16, name="zeros", align_bytes=64)
+
+        def zero(plane, g0, g1):
+            nc.vector.memset(plane[:, g0:g1, :].bitcast(I32), 0)
+
+        def load_act_codes(m, g0, g1):
+            nc.sync.dma_start(
+                out=act_codes[m][:, g0:g1, :].bitcast(I32),
+                in_=act_words[m][g0:g1, :, :].rearrange("g p b -> p g b").bitcast(I32),
+            )
+
+        def load_act_scales(m, g0, g1):
+            for q in range(4):
+                nc.sync.dma_start(
+                    out=act_planes[m][32 * q : 32 * q + 4, g0:g1, :].bitcast(I32),
+                    in_=act_scales[m][g0:g1, 4 * q : 4 * q + 4, :].rearrange("g r n -> r g n").bitcast(I32),
+                )
+
+        def load_wt_codes(s, m, g0, g1):
+            nc.sync.dma_start(
+                out=wt_codes[s % 2][m][:, g0:g1, :].bitcast(I32),
+                in_=wt_words[m][g0:g1, :, 2 * SUPER * s : 2 * SUPER * (s + 1)].rearrange("g p b -> p g b").bitcast(I32),
+            )
+
+        def load_wt_scales(s, m, g0, g1):
+            for q in range(4):
+                nc.sync.dma_start(
+                    out=wt_planes[s % 2][m][32 * q : 32 * q + 4, g0:g1, :].bitcast(I32),
+                    in_=wt_scales[m][g0:g1, 4 * q : 4 * q + 4, SUPER * s : SUPER * (s + 1)].rearrange("g r n -> r g n").bitcast(I32),
+                )
+
+        def load_cn(s):
+            cols = slice(SUPER * s, SUPER * (s + 1))
+            n_tile = cn_pool.tile([P, T_TILES, SUPER], BF16, name="n_tile")
+            nc.sync.dma_start(out=n_tile[:], in_=n[:, cols].rearrange("(t p) f -> p t f", p=P))
+            c_tile = cn_pool.tile([P, T_TILES, SUPER], BF16, name="c_tile")
+            nc.sync.dma_start(out=c_tile[:], in_=c[:, cols].rearrange("(t p) f -> p t f", p=P))
+            return n_tile, c_tile
+
+        def load_super(s):
+            for m in range(2):
+                load_wt_codes(s, m, 0, 4)
+                load_wt_scales(s, m, 0, G)
+                load_wt_codes(s, m, 4, G)
+
+        ratios = {}
+
+        def make_roots(n_tile):
+            roots = []
+            for t in range(T_TILES):
+                y = y_pool.tile([P, SUPER], F32, name="y")
+                nc.scalar.activation(out=y[:], in_=n_tile[:, t, :], func=ACT.Abs_reciprocal_sqrt, bias=EPS)
+                roots.append(y)
+            return roots
+
+        def make_ratios(s, roots, c_tile):
+            for t, y in enumerate(roots):
+                ratio = ratio_pool.tile([P, SUPER], F32, name="ratio")
+                nc.vector.tensor_tensor(out=ratio[:], in0=y[:], in1=c_tile[:, t, :], op=MULT)
+                nc.vector.tensor_tensor(out=ratio[:], in0=ratio[:], in1=y[:], op=MULT)
+                ratios[s, t] = ratio
+
+        def mx_pass(acc, s, t, c0, c1, k):
+            m, g = divmod(k, G)
+            nc.tensor.matmul_mx(
+                out=acc[:, 0 : c1 - c0],
+                lhsT=act_codes[m][:, g, 2 * P * t : 2 * P * (t + 1)].bitcast(FP4X4),
+                lhsT_scale=act_planes[m][:, g, P * t : P * (t + 1)],
+                rhs=wt_codes[s % 2][m][:, g, 2 * c0 : 2 * c1].bitcast(FP4X4),
+                rhs_scale=wt_planes[s % 2][m][:, g, c0:c1],
+                start=(k == 0),
+                stop=(k == 2 * G - 1),
+            )
+
+        def add_bias(v, acc, s, c0, c1):
+            nc.vector.tensor_tensor(out=v[:, c0:c1], in0=acc[:, 0 : c1 - c0], in1=bias_all[:, SUPER * s + c0 : SUPER * s + c1], op=ADD)
+
+        def gate(v, c0, c1):
+            nc.scalar.activation(out=v[:, c0:c1], in_=v[:, c0:c1], func=ACT.Sigmoid)
+
+        def apply_ratio(v, s, t, c0, c1):
+            nc.vector.tensor_tensor(out=v[:, c0:c1], in0=v[:, c0:c1], in1=ratios[s, t][:, c0:c1], op=MULT)
+
+        def store(engine, v, s, t, c0, c1):
+            engine.dma_start(out=out[P * t : P * (t + 1), SUPER * s + c0 : SUPER * s + c1], in_=v[:, c0:c1])
+
+        with tc.manual_schedule():
+            nc.gpsimd.memset(zeros[:], 0.0)
+            warm = psum.tile([P, BANK], F32, name="acc")
+            for i in range(WARM_UP):
+                nc.tensor.matmul(warm[:], lhsT=zeros[:, 0:P], rhs=zeros[:], start=True, stop=True)
+
+            load_act_codes(0, 0, 1)
+            load_wt_codes(0, 0, 0, 1)
+            zero(act_planes[0], 0, 2)
+            zero(wt_planes[0][0], 0, 2)
+            load_act_scales(0, 0, 2)
+            load_wt_scales(0, 0, 0, 2)
+            load_wt_codes(0, 0, 1, 2)
+            load_act_codes(0, 1, 4)
+            load_wt_codes(0, 0, 2, 4)
+            zero(act_planes[0], 2, G)
+            zero(wt_planes[0][0], 2, G)
+            load_act_scales(0, 2, G)
+            load_wt_scales(0, 0, 2, G)
+            load_act_codes(0, 4, G)
+            load_wt_codes(0, 0, 4, G)
+            load_act_codes(1, 0, G)
+            load_wt_codes(0, 1, 0, 4)
+            zero(act_planes[1], 0, G)
+            zero(wt_planes[0][1], 0, G)
+            load_act_scales(1, 0, G)
+            load_wt_scales(0, 1, 0, G)
+            load_wt_codes(0, 1, 4, G)
+            n0, c0_tile = load_cn(0)
+            nc.sync.dma_start(out=bias_all[:], in_=b_o.partition_broadcast(P))
+            n1, c1_tile = load_cn(1)
+            zero(wt_planes[1][0], 0, G)
+            zero(wt_planes[1][1], 0, G)
+            load_super(1)
+
+            accs = {}
+            for t in range(T_TILES):
+                for half in range(HALVES):
+                    acc = psum.tile([P, BANK], F32, name="acc")
+                    accs[t, half] = acc
+            for k in range(2 * G):
+                for t in range(T_TILES):
+                    for half in range(HALVES):
+                        mx_pass(accs[t, half], 0, t, BANK * half, BANK * (half + 1), k)
+            make_ratios(0, make_roots(n0), c0_tile)
+            roots1 = make_roots(n1)
+            vs = {}
+            for t in range(T_TILES):
+                v = v_pool.tile([P, SUPER], F32, name="v")
+                vs[t] = v
+                for half in range(HALVES):
+                    add_bias(v, accs[t, half], 0, BANK * half, BANK * (half + 1))
+                    gate(v, BANK * half, BANK * (half + 1))
+            make_ratios(1, roots1, c1_tile)
+            for t in range(T_TILES):
+                for half in range(HALVES):
+                    apply_ratio(vs[t], 0, t, BANK * half, BANK * (half + 1))
+                store(nc.gpsimd, vs[t], 0, t, 0, SUPER)
+
+            for s in range(1, N_SUPER):
+                if s + 1 < N_SUPER:
+                    n_next, c_next = load_cn(s + 1)
+                    load_super(s + 1)
+                for t in range(T_TILES):
+                    last = s == N_SUPER - 1 and t == T_TILES - 1
+                    cuts = [0, 512, 768, 896, 1024] if last else [0, 512, 1024]
+                    v = v_pool.tile([P, SUPER], F32, name="v")
+                    for c0, c1 in zip(cuts[:-1], cuts[1:]):
+                        acc = psum.tile([P, BANK], F32, name="acc")
+                        for k in range(2 * G):
+                            mx_pass(acc, s, t, c0, c1, k)
+                        add_bias(v, acc, s, c0, c1)
+                        gate(v, c0, c1)
+                        apply_ratio(v, s, t, c0, c1)
+                        if last:
+                            store(nc.sync, v, s, t, c0, c1)
+                    if not last:
+                        store(nc.gpsimd, v, s, t, 0, SUPER)
+                    if t == 0 and s + 1 < N_SUPER:
+                        make_ratios(s + 1, make_roots(n_next), c_next)

@@ -22,6 +22,8 @@ HALVES = SUPER // BANK
 N_SUPER = D // SUPER
 EPS = 1e-6
 WARM_UP = 9
+FIRST_RUNS = ((0, 1), (1, 2), (2, 4), (4, 8), (8, 12), (12, 16))
+RUNS = ((0, 4), (4, 8), (8, 12), (12, 16))
 FLOPS = 2 * TOKENS * D * (2 * D)
 
 
@@ -31,7 +33,7 @@ def tile_slstmcell_pb_kernel(tc, x_words, x_scales, h_words, h_scales, c, n, w_w
         keep = ctx.enter_context(tc.tile_pool(name="keep", bufs=1))
         cn_pool = ctx.enter_context(tc.tile_pool(name="cn", bufs=2))
         y_pool = ctx.enter_context(tc.tile_pool(name="y", bufs=4))
-        ratio_pool = ctx.enter_context(tc.tile_pool(name="ratio", bufs=8))
+        ratio_pool = ctx.enter_context(tc.tile_pool(name="ratio", bufs=4))
         v_pool = ctx.enter_context(tc.tile_pool(name="v", bufs=4))
         psum = ctx.enter_context(tc.psum_pool(name="psum", bufs=8))
 
@@ -50,7 +52,9 @@ def tile_slstmcell_pb_kernel(tc, x_words, x_scales, h_words, h_scales, c, n, w_w
                 planes_b.append(keep.tile([P, G, SUPER], U8, name="wt_planes%d_%d" % (b, m), align_bytes=64))
             wt_codes.append(codes_b)
             wt_planes.append(planes_b)
-        bias_all = keep.tile([P, D], BF16, name="bias_all", align_bytes=64)
+        bias_tiles = []
+        for s in range(N_SUPER):
+            bias_tiles.append(keep.tile([P, SUPER], BF16, name="bias%d" % s, align_bytes=64))
         zeros = keep.tile([P, BANK], BF16, name="zeros", align_bytes=64)
 
         def zero(plane, g0, g1):
@@ -90,11 +94,14 @@ def tile_slstmcell_pb_kernel(tc, x_words, x_scales, h_words, h_scales, c, n, w_w
             nc.sync.dma_start(out=c_tile[:], in_=c[:, cols].rearrange("(t p) f -> p t f", p=P))
             return n_tile, c_tile
 
+        def load_bias(s):
+            nc.sync.dma_start(out=bias_tiles[s][:], in_=b_o[SUPER * s : SUPER * (s + 1)].partition_broadcast(P))
+
         def load_super(s):
             for m in range(2):
                 load_wt_codes(s, m, 0, 4)
-                load_wt_scales(s, m, 0, G)
                 load_wt_codes(s, m, 4, G)
+                load_wt_scales(s, m, 0, G)
 
         ratios = {}
 
@@ -126,7 +133,7 @@ def tile_slstmcell_pb_kernel(tc, x_words, x_scales, h_words, h_scales, c, n, w_w
             )
 
         def add_bias(v, acc, s, c0, c1):
-            nc.vector.tensor_tensor(out=v[:, c0:c1], in0=acc[:, 0 : c1 - c0], in1=bias_all[:, SUPER * s + c0 : SUPER * s + c1], op=ADD)
+            nc.vector.tensor_tensor(out=v[:, c0:c1], in0=acc[:, 0 : c1 - c0], in1=bias_tiles[s][:, c0:c1], op=ADD)
 
         def gate(v, c0, c1):
             nc.scalar.activation(out=v[:, c0:c1], in_=v[:, c0:c1], func=ACT.Sigmoid)
@@ -139,9 +146,6 @@ def tile_slstmcell_pb_kernel(tc, x_words, x_scales, h_words, h_scales, c, n, w_w
 
         with tc.manual_schedule():
             nc.gpsimd.memset(zeros[:], 0.0)
-            warm = psum.tile([P, BANK], F32, name="acc")
-            for i in range(WARM_UP):
-                nc.tensor.matmul(warm[:], lhsT=zeros[:, 0:P], rhs=zeros[:], start=True, stop=True)
 
             load_act_codes(0, 0, 1)
             load_wt_codes(0, 0, 0, 1)
@@ -165,55 +169,63 @@ def tile_slstmcell_pb_kernel(tc, x_words, x_scales, h_words, h_scales, c, n, w_w
             load_act_scales(1, 0, G)
             load_wt_scales(0, 1, 0, G)
             load_wt_codes(0, 1, 4, G)
-            n0, c0_tile = load_cn(0)
-            nc.sync.dma_start(out=bias_all[:], in_=b_o.partition_broadcast(P))
-            n1, c1_tile = load_cn(1)
             zero(wt_planes[1][0], 0, G)
             zero(wt_planes[1][1], 0, G)
+            load_bias(0)
             load_super(1)
+            n_next, c_next = load_cn(0)
+            for s in range(1, N_SUPER):
+                load_bias(s)
 
-            accs = {}
-            for t in range(T_TILES):
-                for half in range(HALVES):
-                    acc = psum.tile([P, BANK], F32, name="acc")
-                    accs[t, half] = acc
-            for k in range(2 * G):
+            warm = psum.tile([P, BANK], F32, name="acc")
+            for i in range(WARM_UP):
+                nc.tensor.matmul(warm[:], lhsT=zeros[:, 0:P], rhs=zeros[:], start=True, stop=True)
+
+            roots = make_roots(n_next)
+
+            for s in range(N_SUPER - 1):
+                runs = FIRST_RUNS if s == 0 else RUNS
+                c_tile = c_next
+                if s > 0:
+                    load_super(s + 1)
+                n_next, c_next = load_cn(s + 1)
+                accs, vs = {}, {}
                 for t in range(T_TILES):
                     for half in range(HALVES):
-                        mx_pass(accs[t, half], 0, t, BANK * half, BANK * (half + 1), k)
-            make_ratios(0, make_roots(n0), c0_tile)
-            roots1 = make_roots(n1)
-            vs = {}
-            for t in range(T_TILES):
-                v = v_pool.tile([P, SUPER], F32, name="v")
-                vs[t] = v
-                for half in range(HALVES):
-                    add_bias(v, accs[t, half], 0, BANK * half, BANK * (half + 1))
-                    gate(v, BANK * half, BANK * (half + 1))
-            make_ratios(1, roots1, c1_tile)
-            for t in range(T_TILES):
-                for half in range(HALVES):
-                    apply_ratio(vs[t], 0, t, BANK * half, BANK * (half + 1))
-                store(nc.gpsimd, vs[t], 0, t, 0, SUPER)
-
-            for s in range(1, N_SUPER):
-                if s + 1 < N_SUPER:
-                    n_next, c_next = load_cn(s + 1)
-                    load_super(s + 1)
-                for t in range(T_TILES):
-                    last = s == N_SUPER - 1 and t == T_TILES - 1
-                    cuts = [0, 512, 768, 896, 1024] if last else [0, 512, 1024]
-                    v = v_pool.tile([P, SUPER], F32, name="v")
-                    for c0, c1 in zip(cuts[:-1], cuts[1:]):
                         acc = psum.tile([P, BANK], F32, name="acc")
-                        for k in range(2 * G):
-                            mx_pass(acc, s, t, c0, c1, k)
-                        add_bias(v, acc, s, c0, c1)
-                        gate(v, c0, c1)
-                        apply_ratio(v, s, t, c0, c1)
-                        if last:
-                            store(nc.sync, v, s, t, c0, c1)
-                    if not last:
-                        store(nc.gpsimd, v, s, t, 0, SUPER)
-                    if t == 0 and s + 1 < N_SUPER:
-                        make_ratios(s + 1, make_roots(n_next), c_next)
+                        accs[t, half] = acc
+                for k0, k1 in runs:
+                    for t in range(T_TILES):
+                        for k in range(k0, k1):
+                            for half in range(HALVES):
+                                mx_pass(accs[t, half], s, t, BANK * half, BANK * (half + 1), k)
+                for t in range(T_TILES):
+                    v = v_pool.tile([P, SUPER], F32, name="v")
+                    vs[t] = v
+                    for half in range(HALVES):
+                        add_bias(v, accs[t, half], s, BANK * half, BANK * (half + 1))
+                        gate(v, BANK * half, BANK * (half + 1))
+                if s == 0:
+                    make_ratios(0, roots, c_tile)
+                for t in range(T_TILES):
+                    for half in range(HALVES):
+                        apply_ratio(vs[t], s, t, BANK * half, BANK * (half + 1))
+                    store(nc.gpsimd, vs[t], s, t, 0, SUPER)
+                make_ratios(s + 1, make_roots(n_next), c_next)
+
+            s = N_SUPER - 1
+            for t in range(T_TILES):
+                last = t == T_TILES - 1
+                cuts = [0, 512, 768, 896, 1024] if last else [0, 512, 1024]
+                v = v_pool.tile([P, SUPER], F32, name="v")
+                for c0, c1 in zip(cuts[:-1], cuts[1:]):
+                    acc = psum.tile([P, BANK], F32, name="acc")
+                    for k in range(2 * G):
+                        mx_pass(acc, s, t, c0, c1, k)
+                    add_bias(v, acc, s, c0, c1)
+                    gate(v, c0, c1)
+                    apply_ratio(v, s, t, c0, c1)
+                    if last:
+                        store(nc.sync, v, s, t, c0, c1)
+                if not last:
+                    store(nc.gpsimd, v, s, t, 0, SUPER)

@@ -22,7 +22,7 @@ HALVES = SUPER // BANK
 N_SUPER = D // SUPER
 EPS = 1e-6
 WARM_UP = 9
-FIRST_RUNS = ((0, 1), (1, 2), (2, 4), (4, 8), (8, 12), (12, 16))
+FIRST_RUNS = ((0, 1), (1, 2), (2, 3), (3, 4), (4, 6), (6, 8), (8, 10), (10, 12), (12, 16))
 RUNS = ((0, 4), (4, 8), (8, 12), (12, 16))
 FLOPS = 2 * TOKENS * D * (2 * D)
 
@@ -99,9 +99,9 @@ def tile_slstmcell_pb_kernel(tc, x_words, x_scales, h_words, h_scales, c, n, w_w
 
         def load_super(s):
             for m in range(2):
-                load_wt_codes(s, m, 0, 4)
-                load_wt_codes(s, m, 4, G)
-                load_wt_scales(s, m, 0, G)
+                for g in (0, 4):
+                    load_wt_scales(s, m, g, g + 4)
+                    load_wt_codes(s, m, g, g + 4)
 
         ratios = {}
 
@@ -154,21 +154,22 @@ def tile_slstmcell_pb_kernel(tc, x_words, x_scales, h_words, h_scales, c, n, w_w
             load_act_scales(0, 0, 2)
             load_wt_scales(0, 0, 0, 2)
             load_wt_codes(0, 0, 1, 2)
-            load_act_codes(0, 1, 4)
-            load_wt_codes(0, 0, 2, 4)
-            zero(act_planes[0], 2, G)
-            zero(wt_planes[0][0], 2, G)
-            load_act_scales(0, 2, G)
-            load_wt_scales(0, 0, 2, G)
-            load_act_codes(0, 4, G)
-            load_wt_codes(0, 0, 4, G)
-            load_act_codes(1, 0, G)
-            load_wt_codes(0, 1, 0, 4)
-            zero(act_planes[1], 0, G)
-            zero(wt_planes[0][1], 0, G)
-            load_act_scales(1, 0, G)
-            load_wt_scales(0, 1, 0, G)
-            load_wt_codes(0, 1, 4, G)
+            load_act_codes(0, 1, 2)
+            zero(wt_planes[0][0], 2, 4)
+            zero(act_planes[0], 2, 4)
+            load_wt_scales(0, 0, 2, 4)
+            load_act_scales(0, 2, 4)
+            load_wt_codes(0, 0, 2, 3)
+            load_act_codes(0, 2, 4)
+            load_wt_codes(0, 0, 3, 4)
+            for m, first in ((0, 4), (1, 0), (1, 4)):
+                zero(wt_planes[0][m], first, first + 4)
+                zero(act_planes[m], first, first + 4)
+                load_wt_scales(0, m, first, first + 4)
+                load_act_scales(m, first, first + 4)
+                for g in (first, first + 2):
+                    load_wt_codes(0, m, g, g + 2)
+                    load_act_codes(m, g, g + 2)
             zero(wt_planes[1][0], 0, G)
             zero(wt_planes[1][1], 0, G)
             load_bias(0)

from contextlib import ExitStack

import concourse.mybir as mybir

F32 = mybir.dt.float32
BF16 = mybir.dt.bfloat16
U8 = mybir.dt.uint8
I32 = mybir.dt.int32
FP4X4 = mybir.dt.float4_e2m1fn_x4
ADD = mybir.AluOpType.add
MULT = mybir.AluOpType.mult
ACT = mybir.ActivationFunctionType

P = 128
TOKENS = 512
D = 4096
G = 8
T_TILES = TOKENS // P
BANK = 512
SUPER = 1024
HALVES = SUPER // BANK
N_SUPER = D // SUPER
EPS = 1e-6
WARM_UP = 9
FIRST_RUNS = ((0, 1), (1, 2), (2, 3), (3, 4), (4, 6), (6, 8), (8, 10), (10, 12), (12, 16))
RUNS = ((0, 4), (4, 8), (8, 12), (12, 16))
FLOPS = 2 * TOKENS * D * (2 * D)


def tile_slstmcell_pb_kernel(tc, x_words, x_scales, h_words, h_scales, c, n, w_words, w_scales, b_o, u_words, u_scales, out):
    nc = tc.nc
    with ExitStack() as ctx:
        keep = ctx.enter_context(tc.tile_pool(name="keep", bufs=1))
        cn_pool = ctx.enter_context(tc.tile_pool(name="cn", bufs=2))
        y_pool = ctx.enter_context(tc.tile_pool(name="y", bufs=4))
        ratio_pool = ctx.enter_context(tc.tile_pool(name="ratio", bufs=4))
        v_pool = ctx.enter_context(tc.tile_pool(name="v", bufs=4))
        psum = ctx.enter_context(tc.psum_pool(name="psum", bufs=8))

        act_words = (x_words, h_words)
        act_scales = (x_scales, h_scales)
        wt_words = (w_words, u_words)
        wt_scales = (w_scales, u_scales)
        act_codes, act_planes, wt_codes, wt_planes = [], [], [], []
        for m in range(2):
            act_codes.append(keep.tile([P, G, 2 * TOKENS], U8, name="act_codes%d" % m, align_bytes=64))
            act_planes.append(keep.tile([P, G, TOKENS], U8, name="act_planes%d" % m, align_bytes=64))
        for b in range(2):
            codes_b, planes_b = [], []
            for m in range(2):
                codes_b.append(keep.tile([P, G, 2 * SUPER], U8, name="wt_codes%d_%d" % (b, m), align_bytes=64))
                planes_b.append(keep.tile([P, G, SUPER], U8, name="wt_planes%d_%d" % (b, m), align_bytes=64))
            wt_codes.append(codes_b)
            wt_planes.append(planes_b)
        bias_tiles = []
        for s in range(N_SUPER):
            bias_tiles.append(keep.tile([P, SUPER], BF16, name="bias%d" % s, align_bytes=64))
        zeros = keep.tile([P, BANK], BF16, name="zeros", align_bytes=64)

        def zero(plane, g0, g1):
            nc.vector.memset(plane[:, g0:g1, :].bitcast(I32), 0)

        def load_act_codes(m, g0, g1):
            nc.sync.dma_start(
                out=act_codes[m][:, g0:g1, :].bitcast(I32),
                in_=act_words[m][g0:g1, :, :].rearrange("g p b -> p g b").bitcast(I32),
            )

        def load_act_scales(m, g0, g1):
            for q in range(4):
                nc.sync.dma_start(
                    out=act_planes[m][32 * q : 32 * q + 4, g0:g1, :].bitcast(I32),
                    in_=act_scales[m][g0:g1, 4 * q : 4 * q + 4, :].rearrange("g r n -> r g n").bitcast(I32),
                )

        def load_wt_codes(s, m, g0, g1):
            nc.sync.dma_start(
                out=wt_codes[s % 2][m][:, g0:g1, :].bitcast(I32),
                in_=wt_words[m][g0:g1, :, 2 * SUPER * s : 2 * SUPER * (s + 1)].rearrange("g p b -> p g b").bitcast(I32),
            )

        def load_wt_scales(s, m, g0, g1):
            for q in range(4):
                nc.sync.dma_start(
                    out=wt_planes[s % 2][m][32 * q : 32 * q + 4, g0:g1, :].bitcast(I32),
                    in_=wt_scales[m][g0:g1, 4 * q : 4 * q + 4, SUPER * s : SUPER * (s + 1)].rearrange("g r n -> r g n").bitcast(I32),
                )

        def load_cn(s):
            cols = slice(SUPER * s, SUPER * (s + 1))
            n_tile = cn_pool.tile([P, T_TILES, SUPER], BF16, name="n_tile")
            nc.sync.dma_start(out=n_tile[:], in_=n[:, cols].rearrange("(t p) f -> p t f", p=P))
            c_tile = cn_pool.tile([P, T_TILES, SUPER], BF16, name="c_tile")
            nc.sync.dma_start(out=c_tile[:], in_=c[:, cols].rearrange("(t p) f -> p t f", p=P))
            return n_tile, c_tile

        def load_bias(s):
            nc.sync.dma_start(out=bias_tiles[s][:], in_=b_o[SUPER * s : SUPER * (s + 1)].partition_broadcast(P))

        def load_super(s):
            for m in range(2):
                for g in (0, 4):
                    load_wt_scales(s, m, g, g + 4)
                    load_wt_codes(s, m, g, g + 4)

        ratios = {}

        def make_roots(n_tile):
            roots = []
            for t in range(T_TILES):
                y = y_pool.tile([P, SUPER], F32, name="y")
                nc.scalar.activation(out=y[:], in_=n_tile[:, t, :], func=ACT.Abs_reciprocal_sqrt, bias=EPS)
                roots.append(y)
            return roots

        def make_ratios(s, roots, c_tile):
            for t, y in enumerate(roots):
                ratio = ratio_pool.tile([P, SUPER], F32, name="ratio")
                nc.vector.tensor_tensor(out=ratio[:], in0=y[:], in1=c_tile[:, t, :], op=MULT)
                nc.vector.tensor_tensor(out=ratio[:], in0=ratio[:], in1=y[:], op=MULT)
                ratios[s, t] = ratio

        def mx_pass(acc, s, t, c0, c1, k):
            m, g = divmod(k, G)
            nc.tensor.matmul_mx(
                out=acc[:, 0 : c1 - c0],
                lhsT=act_codes[m][:, g, 2 * P * t : 2 * P * (t + 1)].bitcast(FP4X4),
                lhsT_scale=act_planes[m][:, g, P * t : P * (t + 1)],
                rhs=wt_codes[s % 2][m][:, g, 2 * c0 : 2 * c1].bitcast(FP4X4),
                rhs_scale=wt_planes[s % 2][m][:, g, c0:c1],
                start=(k == 0),
                stop=(k == 2 * G - 1),
            )

        def add_bias(v, acc, s, c0, c1):
            nc.vector.tensor_tensor(out=v[:, c0:c1], in0=acc[:, 0 : c1 - c0], in1=bias_tiles[s][:, c0:c1], op=ADD)

        def gate(v, c0, c1):
            nc.scalar.activation(out=v[:, c0:c1], in_=v[:, c0:c1], func=ACT.Sigmoid)

        def apply_ratio(v, s, t, c0, c1):
            nc.vector.tensor_tensor(out=v[:, c0:c1], in0=v[:, c0:c1], in1=ratios[s, t][:, c0:c1], op=MULT)

        def store(engine, v, s, t, c0, c1):
            engine.dma_start(out=out[P * t : P * (t + 1), SUPER * s + c0 : SUPER * s + c1], in_=v[:, c0:c1])

        with tc.manual_schedule():
            nc.gpsimd.memset(zeros[:], 0.0)

            load_act_codes(0, 0, 1)
            load_wt_codes(0, 0, 0, 1)
            zero(act_planes[0], 0, 2)
            zero(wt_planes[0][0], 0, 2)
            load_act_scales(0, 0, 2)
            load_wt_scales(0, 0, 0, 2)
            load_wt_codes(0, 0, 1, 2)
            load_act_codes(0, 1, 2)
            zero(wt_planes[0][0], 2, 4)
            zero(act_planes[0], 2, 4)
            load_wt_scales(0, 0, 2, 4)
            load_act_scales(0, 2, 4)
            load_wt_codes(0, 0, 2, 3)
            load_act_codes(0, 2, 4)
            load_wt_codes(0, 0, 3, 4)
            for m, first in ((0, 4), (1, 0), (1, 4)):
                zero(wt_planes[0][m], first, first + 4)
                zero(act_planes[m], first, first + 4)
                load_wt_scales(0, m, first, first + 4)
                load_act_scales(m, first, first + 4)
                for g in (first, first + 2):
                    load_wt_codes(0, m, g, g + 2)
                    load_act_codes(m, g, g + 2)
            zero(wt_planes[1][0], 0, G)
            zero(wt_planes[1][1], 0, G)
            load_bias(0)
            load_super(1)
            n_next, c_next = load_cn(0)
            for s in range(1, N_SUPER):
                load_bias(s)

            warm = psum.tile([P, BANK], F32, name="acc")
            for i in range(WARM_UP):
                nc.tensor.matmul(warm[:], lhsT=zeros[:, 0:P], rhs=zeros[:], start=True, stop=True)

            roots = make_roots(n_next)

            for s in range(N_SUPER - 1):
                runs = FIRST_RUNS if s == 0 else RUNS
                c_tile = c_next
                if s > 0:
                    load_super(s + 1)
                n_next, c_next = load_cn(s + 1)
                accs, vs = {}, {}
                for t in range(T_TILES):
                    for half in range(HALVES):
                        acc = psum.tile([P, BANK], F32, name="acc")
                        accs[t, half] = acc
                for k0, k1 in runs:
                    for t in range(T_TILES):
                        for k in range(k0, k1):
                            for half in range(HALVES):
                                mx_pass(accs[t, half], s, t, BANK * half, BANK * (half + 1), k)
                for t in range(T_TILES):
                    v = v_pool.tile([P, SUPER], F32, name="v")
                    vs[t] = v
                    for half in range(HALVES):
                        add_bias(v, accs[t, half], s, BANK * half, BANK * (half + 1))
                        gate(v, BANK * half, BANK * (half + 1))
                if s == 0:
                    make_ratios(0, roots, c_tile)
                for t in range(T_TILES):
                    for half in range(HALVES):
                        apply_ratio(vs[t], s, t, BANK * half, BANK * (half + 1))
                    store(nc.gpsimd, vs[t], s, t, 0, SUPER)
                make_ratios(s + 1, make_roots(n_next), c_next)

            s = N_SUPER - 1
            for t in range(T_TILES):
                last = t == T_TILES - 1
                cuts = [0, 512, 768, 896, 1024] if last else [0, 512, 1024]
                v = v_pool.tile([P, SUPER], F32, name="v")
                for c0, c1 in zip(cuts[:-1], cuts[1:]):
                    acc = psum.tile([P, BANK], F32, name="acc")
                    for k in range(2 * G):
                        mx_pass(acc, s, t, c0, c1, k)
                    add_bias(v, acc, s, c0, c1)
                    gate(v, c0, c1)
                    apply_ratio(v, s, t, c0, c1)
                    if last:
                        store(nc.sync, v, s, t, c0, c1)
                if not last:
                    store(nc.gpsimd, v, s, t, 0, SUPER)
